import numpy as np
import ml_dtypes


def mxq(x, axis, fmt="e4m3"):
    dtype, down = {"e4m3": (ml_dtypes.float8_e4m3fn, 7), "e5m2": (ml_dtypes.float8_e5m2, 14)}[fmt]
    v = np.moveaxis(np.asarray(x, np.float32).astype(ml_dtypes.bfloat16).astype(np.float64), axis, -1)
    blocks = v.reshape(v.shape[:-1] + (-1, 32))
    amax = np.abs(blocks).max(-1, keepdims=True)
    byte = np.maximum(np.where(amax > 0, np.frexp(amax)[1] - 1 + 127, 0) - down, 1)
    scale = np.exp2(byte - 127.0)
    codes = (blocks / scale).astype(np.float32).astype(dtype).astype(np.float64)
    return np.moveaxis((codes * scale).reshape(v.shape), -1, axis)


WIDE = False


def mx_kscale(k):
    if not WIDE:
        return np.ones(k)
    levels = np.array([10, -10, 5, -5, 0])
    a = np.random.permutation(np.resize(levels, k // 512 * 4)).reshape(k // 512, 4)
    idx = np.arange(k)
    return np.exp2(a[idx // 512, idx % 128 // 32])


BF16 = ml_dtypes.bfloat16


def bf(x):
    return np.asarray(x, np.float32).astype(BF16)


def f64(x):
    return np.asarray(x).astype(np.float64)


N, DB, DV, DL, DC, T, DO = 2048, 500, 1012, 256, 128, 12, 256
KB, KV = DB + T, DV + T
LN_EPS = 1e-5
ERF_TERMS = 100


def erf(v):
    a = np.clip(v, -6.0, 6.0)
    term = a.copy()
    tot = a.copy()
    for n in range(1, ERF_TERMS):
        term = term * (2.0 * a * a) / (2.0 * n + 1.0)
        tot = tot + term
    return 2.0 / np.sqrt(np.pi) * np.exp(-a * a) * tot


def gelu_erf(v):
    return 0.5 * v * (1.0 + erf(v / np.sqrt(2.0)))


def t2v(t, w0, w, b):
    v0 = w0 * t + b[0]
    v = np.sin(w * t[:, None] + b[1:])
    return np.concatenate([v0[:, None], v], axis=-1)


def branch(z, gamma, beta, W):
    mu = z.mean(-1, keepdims=True)
    var = np.square(z - mu).mean(-1, keepdims=True)
    zn = (z - mu) / np.sqrt(var + LN_EPS) * gamma + beta
    return gelu_erf(mxq(zn, 1, "e4m3") @ mxq(W, 0, "e4m3"))


def rows(d):
    return np.random.standard_normal((N, d)) * (0.5 + np.random.uniform(size=(N, 1))) + 0.3 * np.random.standard_normal((N, 1))


def setup_inputs():
    sb, sv = mx_kscale(KB), mx_kscale(KV)
    return {"x_bill": bf(rows(DB)), "ts_bill": bf(np.random.uniform(size=N)),
            "x_bill_version": bf(rows(DV)), "ts_bill_version": bf(np.random.uniform(size=N)),
            "w0": bf(3.0 + 0.5 * np.random.standard_normal(1)),
            "w": bf(3.0 * np.random.standard_normal(T - 1)),
            "b": bf(1.5 + 0.5 * np.random.standard_normal(T)),
            "gamma_bill": bf((1.0 + 0.1 * np.random.standard_normal(KB)) * sb),
            "beta_bill": bf(0.1 * np.random.standard_normal(KB) * sb),
            "W_bill": bf(np.random.standard_normal((KB, DO)) * np.sqrt(2.0 / KB) / sb[:, None]),
            "gamma_bill_version": bf((1.0 + 0.1 * np.random.standard_normal(KV)) * sv),
            "beta_bill_version": bf(0.1 * np.random.standard_normal(KV) * sv),
            "W_bill_version": bf(np.random.standard_normal((KV, DO)) * np.sqrt(2.0 / KV) / sv[:, None])}


def reference(x_bill, ts_bill, x_bill_version, ts_bill_version, w0, w, b,
              gamma_bill, beta_bill, W_bill, gamma_bill_version, beta_bill_version, W_bill_version):
    w0, w, b = f64(w0), f64(w), f64(b)
    zb = np.concatenate([f64(x_bill), t2v(f64(ts_bill), w0, w, b)], axis=1)
    zv = np.concatenate([f64(x_bill_version), t2v(f64(ts_bill_version), w0, w, b)], axis=1)
    out_bill = branch(zb, f64(gamma_bill), f64(beta_bill), f64(W_bill))
    out_bv = branch(zv, f64(gamma_bill_version), f64(beta_bill_version), f64(W_bill_version))
    return np.stack([out_bill, out_bv], axis=0)

@@ -1,0 +1,341 @@
+from contextlib import ExitStack
+import math
+
+import concourse.mybir as mybir
+from concourse.masks import make_identity
+
+F32 = mybir.dt.float32
+BF16 = mybir.dt.bfloat16
+U32 = mybir.dt.uint32
+U8 = mybir.dt.uint8
+FP8X4 = mybir.dt.float8_e4m3fn_x4
+ACT = mybir.ActivationFunctionType
+ALU = mybir.AluOpType
+
+P = 128
+PACK = 4
+K_PASS = P * PACK
+ROWS = 2048
+ROW_TILES = ROWS // P
+GROUP = 4
+GROUPS = ROW_TILES // GROUP
+GROUP_COLS = GROUP * P
+T2V = 12
+D_OUT = 256
+LN_EPS = 1e-5
+BN_MAX = 512
+BN_DIM = 6
+KINDS = 2
+
+ROUND_MAGIC = 12582912.0
+TWO_PI_HIGH = 6.28125
+TWO_PI_LOW = 2.0 * math.pi - TWO_PI_HIGH
+SIN_LIMIT = 3.1415925
+
+SCALAR_NORM_TILES = 2
+
+FLOPS = 2 * ROWS * D_OUT * (512 + 1024)
+
+
+def tile_featureprojector_pa_kernel(
+    tc,
+    x_bill,
+    ts_bill,
+    x_bill_version,
+    ts_bill_version,
+    w0,
+    w,
+    b,
+    gamma_bill,
+    beta_bill,
+    W_bill,
+    gamma_bill_version,
+    beta_bill_version,
+    W_bill_version,
+    out,
+):
+    nc = tc.nc
+    kinds = [
+        {"x": x_bill, "ts": ts_bill, "gamma": gamma_bill, "beta": beta_bill, "W": W_bill, "first": 0},
+        {
+            "x": x_bill_version,
+            "ts": ts_bill_version,
+            "gamma": gamma_bill_version,
+            "beta": beta_bill_version,
+            "W": W_bill_version,
+            "first": 4,
+        },
+    ]
+    for kind in kinds:
+        kind["d"] = kind["x"].shape[1]
+        kind["k"] = kind["d"] + T2V
+        kind["tiles"] = kind["k"] // P
+        kind["passes"] = kind["k"] // K_PASS
+        kind["chunks"] = (kind["d"] + BN_MAX - 1) // BN_MAX
+    all_tiles = sum(kind["tiles"] for kind in kinds)
+    all_passes = sum(kind["passes"] for kind in kinds)
+
+    with ExitStack() as stack:
+        const = stack.enter_context(tc.tile_pool(name="const", bufs=1))
+        x_pool = stack.enter_context(tc.tile_pool(name="x", bufs=1))
+        small = stack.enter_context(tc.tile_pool(name="small", bufs=4))
+        xn_pool = stack.enter_context(tc.tile_pool(name="xn", bufs=2))
+        work = stack.enter_context(tc.tile_pool(name="work", bufs=4))
+        turned_pool = stack.enter_context(tc.psum_pool(name="turned", bufs=6))
+        acc_pool = stack.enter_context(tc.psum_pool(name="acc", bufs=2))
+
+        ts_sb = const.tile([P, KINDS, ROW_TILES], BF16)
+        for j, kind in enumerate(kinds):
+            nc.sync.dma_start(out=ts_sb[:, j, :], in_=kind["ts"].rearrange("(p i) -> p i", i=ROW_TILES))
+        w0_sb = const.tile([P, 1], BF16)
+        nc.sync.dma_start(out=w0_sb[:], in_=w0.partition_broadcast(P))
+        w_sb = const.tile([P, T2V - 1], BF16)
+        nc.sync.dma_start(out=w_sb[:], in_=w.partition_broadcast(P))
+        b_sb = const.tile([P, T2V], BF16)
+        nc.sync.dma_start(out=b_sb[:], in_=b.partition_broadcast(P))
+
+        groups = [(j, g) for j in range(KINDS) for g in range(GROUPS)]
+        x_sb = {}
+
+        def load_rows(j, g):
+            x_tile = x_pool.tile([P, GROUP, kinds[j]["d"]], BF16, name="x_%d_%d" % (j, g))
+            rows = kinds[j]["x"].rearrange("(p i) d -> p i d", i=ROW_TILES)
+            nc.sync.dma_start(out=x_tile[:], in_=rows[:, g * GROUP : (g + 1) * GROUP, :])
+            x_sb[(j, g)] = x_tile
+
+        load_rows(*groups[0])
+
+        gb_rows = const.tile([P, P], BF16)
+        nc.vector.memset(gb_rows[:], 0.0)
+        w_raw = const.tile([P, all_tiles, D_OUT], BF16)
+        for kind in kinds:
+            first, tiles = kind["first"], kind["tiles"]
+            nc.sync.dma_start(out=gb_rows[first : first + tiles, :], in_=kind["gamma"].rearrange("(t p) -> t p", p=P))
+            nc.sync.dma_start(
+                out=gb_rows[all_tiles + first : all_tiles + first + tiles, :],
+                in_=kind["beta"].rearrange("(t p) -> t p", p=P),
+            )
+        for kind in kinds:
+            first, tiles = kind["first"], kind["tiles"]
+            nc.sync.dma_start(out=w_raw[:, first : first + tiles, :], in_=kind["W"].rearrange("(t p) n -> p t n", p=P))
+
+        for j, g in groups[1:]:
+            load_rows(j, g)
+
+        identity = const.tile([P, P], F32)
+        make_identity(nc, identity[:])
+
+        n_ts = KINDS * ROW_TILES
+        n_sin = T2V - 1
+        ts_flat = ts_sb[:].rearrange("p j i -> p (j i)")
+        linear = const.tile([P, n_ts], F32)
+        nc.vector.tensor_scalar(
+            out=linear[:], in0=ts_flat, scalar1=w0_sb[:, 0:1], scalar2=b_sb[:, 0:1], op0=ALU.mult, op1=ALU.add
+        )
+        phase = const.tile([P, n_ts, n_sin], F32)
+        nc.vector.tensor_tensor(
+            out=phase[:],
+            in0=ts_flat.unsqueeze(2).to_broadcast([P, n_ts, n_sin]),
+            in1=w_sb[:].unsqueeze(1).to_broadcast([P, n_ts, n_sin]),
+            op=ALU.mult,
+        )
+        nc.vector.tensor_tensor(
+            out=phase[:], in0=phase[:], in1=b_sb[:, 1:T2V].unsqueeze(1).to_broadcast([P, n_ts, n_sin]), op=ALU.add
+        )
+        phase_flat = phase[:].rearrange("p n s -> p (n s)")
+        turns = const.tile([P, n_ts * n_sin], F32)
+        nc.vector.tensor_scalar(
+            out=turns[:], in0=phase_flat, scalar1=1.0 / (2.0 * math.pi), scalar2=ROUND_MAGIC, op0=ALU.mult, op1=ALU.add
+        )
+        nc.vector.tensor_scalar(out=turns[:], in0=turns[:], scalar1=ROUND_MAGIC, scalar2=None, op0=ALU.subtract)
+        reduced = const.tile([P, n_ts, n_sin], F32)
+        reduced_flat = reduced[:].rearrange("p n s -> p (n s)")
+        nc.vector.scalar_tensor_tensor(
+            out=reduced_flat, in0=turns[:], scalar=-TWO_PI_HIGH, in1=phase_flat, op0=ALU.mult, op1=ALU.add
+        )
+        nc.vector.scalar_tensor_tensor(
+            out=reduced_flat, in0=turns[:], scalar=-TWO_PI_LOW, in1=reduced_flat, op0=ALU.mult, op1=ALU.add
+        )
+        nc.vector.tensor_scalar(
+            out=reduced_flat, in0=reduced_flat, scalar1=-SIN_LIMIT, scalar2=SIN_LIMIT, op0=ALU.max, op1=ALU.min
+        )
+        t2v = const.tile([P, n_ts, T2V], F32)
+        nc.scalar.activation(out=t2v[:, :, 1:T2V], in_=reduced[:], func=ACT.Sin)
+        nc.scalar.copy(out=t2v[:, :, 0:1], in_=linear[:].unsqueeze(2))
+
+        neg_half = const.tile([P, GROUP], F32)
+        nc.vector.memset(neg_half[:], -0.5)
+
+        gamma_beta = const.tile([P, 2 * all_tiles], F32)
+        w_codes = const.tile([P, all_passes, D_OUT], U32, align_bytes=64)
+        w_scales = const.tile([P, all_passes, D_OUT], U8, align_bytes=64)
+
+        def turn_gamma_beta():
+            gb_rows_f32 = const.tile([P, P], F32)
+            nc.vector.tensor_copy(out=gb_rows_f32[:], in_=gb_rows[:])
+            gb_turned = turned_pool.tile([P, GROUP_COLS], F32, tag="turned")
+            nc.tensor.transpose(gb_turned[:, 0:P], gb_rows_f32[:], identity[:])
+            nc.vector.tensor_copy(out=gamma_beta[:], in_=gb_turned[:, 0 : 2 * all_tiles])
+
+        def quantise_w():
+            w_grouped = const.tile([P, all_passes, D_OUT, PACK], BF16, align_bytes=64)
+            for c in range(all_passes):
+                nc.scalar.copy(
+                    out=w_grouped[:, c, :, :], in_=w_raw[:, c * PACK : (c + 1) * PACK, :].rearrange("p t n -> p n t")
+                )
+            for c in range(all_passes):
+                nc.vector.quantize_mx(
+                    out=w_codes[:, c, :].bitcast(FP8X4),
+                    scales=w_scales[:, c, :],
+                    in_=w_grouped[:, c, :, :].rearrange("p n t -> p (n t)"),
+                )
+
+        row_scale = {}
+        row_shift = {}
+        normalised = {}
+        planes = {}
+        zn_codes = {}
+        zn_scales = {}
+        sums = {}
+
+        def statistics(j, g):
+            kind = kinds[j]
+            chunks = kind["chunks"]
+            width = kind["d"] // chunks
+            stats = small.tile([P, GROUP, chunks + 1, BN_DIM], F32, tag="stats")
+            mean_var = small.tile([P, GROUP, 2], F32, tag="mean_var")
+            for i in range(GROUP):
+                for h in range(chunks):
+                    nc.vector.bn_stats(out=stats[:, i, h, :], in_=x_sb[(j, g)][:, i, h * width : (h + 1) * width])
+            for i in range(GROUP):
+                nc.vector.bn_stats(out=stats[:, i, chunks, :], in_=t2v[:, j * ROW_TILES + g * GROUP + i, :])
+            for i in range(GROUP):
+                nc.vector.bn_aggr(out=mean_var[:, i, :], in_=stats[:, i, :, :].rearrange("p h s -> p (h s)"))
+            var_eps = small.tile([P, GROUP], F32, tag="var_eps")
+            nc.gpsimd.tensor_scalar(
+                out=var_eps[:], in0=mean_var[:, :, 1], scalar1=LN_EPS, scalar2=1.0, op0=ALU.add, op1=ALU.mult
+            )
+            scale = small.tile([P, GROUP], F32, tag="scale")
+            nc.gpsimd.tensor_tensor(out=scale[:], in0=var_eps[:], in1=neg_half[:], op=ALU.pow)
+            mean_scaled = small.tile([P, GROUP], F32, tag="mean_scaled")
+            nc.gpsimd.tensor_tensor(out=mean_scaled[:], in0=mean_var[:, :, 0], in1=scale[:], op=ALU.mult)
+            shift = small.tile([P, GROUP], F32, tag="shift")
+            nc.gpsimd.tensor_scalar(
+                out=shift[:], in0=mean_scaled[:], scalar1=-1.0, scalar2=0.0, op0=ALU.mult, op1=ALU.add
+            )
+            row_scale[(j, g)] = scale
+            row_shift[(j, g)] = shift
+
+        def normalise(j, g):
+            kind = kinds[j]
+            d, k = kind["d"], kind["k"]
+            scale, shift = row_scale[(j, g)], row_shift[(j, g)]
+            xn = xn_pool.tile([P, GROUP, k], F32, tag="xn")
+            for i in range(GROUP):
+                parts = [
+                    (xn[:, i, 0:d], x_sb[(j, g)][:, i, :]),
+                    (xn[:, i, d:k], t2v[:, j * ROW_TILES + g * GROUP + i, :]),
+                ]
+                for dst, src in parts:
+                    if i < SCALAR_NORM_TILES:
+                        nc.scalar.activation(
+                            out=dst, in_=src, func=ACT.Identity, scale=scale[:, i : i + 1], bias=shift[:, i : i + 1]
+                        )
+                    else:
+                        nc.vector.tensor_scalar(
+                            out=dst,
+                            in0=src,
+                            scalar1=scale[:, i : i + 1],
+                            scalar2=shift[:, i : i + 1],
+                            op0=ALU.mult,
+                            op1=ALU.add,
+                        )
+            normalised[(j, g)] = xn
+
+        def turn(j, g):
+            kind = kinds[j]
+            xn = normalised[(j, g)]
+            for c in range(kind["passes"]):
+                zn_planes = work.tile([P, PACK, GROUP_COLS], BF16, tag="zn_planes")
+                for t in range(PACK):
+                    tile_in_kind = c * PACK + t
+                    turned = turned_pool.tile([P, GROUP_COLS], F32, tag="turned")
+                    for i in range(GROUP):
+                        nc.tensor.transpose(
+                            turned[:, i * P : (i + 1) * P],
+                            xn[:, i, tile_in_kind * P : (tile_in_kind + 1) * P],
+                            identity[:],
+                        )
+                    col = kind["first"] + tile_in_kind
+                    nc.scalar.activation(
+                        out=zn_planes[:, t, :],
+                        in_=turned[:],
+                        func=ACT.Identity,
+                        scale=gamma_beta[:, col : col + 1],
+                        bias=gamma_beta[:, all_tiles + col : all_tiles + col + 1],
+                    )
+                planes[(j, g, c)] = zn_planes
+
+        def quantise(j, g):
+            passes = kinds[j]["passes"]
+            grouped = {}
+            for c in range(passes):
+                grouped[c] = work.tile([P, GROUP_COLS, PACK], BF16, tag="grouped", align_bytes=64, name="grouped")
+                nc.vector.tensor_copy(
+                    out=grouped[c][:].rearrange("p (n r) t -> p n t r", r=4),
+                    in_=planes[(j, g, c)][:].rearrange("p t (n r) -> p n t r", r=4),
+                )
+            for c in range(passes):
+                zn_codes[(j, g, c)] = work.tile([P, GROUP_COLS], U32, tag="codes", align_bytes=64, name="codes")
+                zn_scales[(j, g, c)] = work.tile([P, GROUP_COLS], U8, tag="scales", align_bytes=64, name="scales")
+                nc.vector.quantize_mx(
+                    out=zn_codes[(j, g, c)][:].bitcast(FP8X4),
+                    scales=zn_scales[(j, g, c)][:],
+                    in_=grouped[c][:].rearrange("p n t -> p (n t)"),
+                )
+
+        def multiply(j, g):
+            passes = kinds[j]["passes"]
+            first_pass = kinds[j]["first"] // PACK
+            for half in range(GROUP // 2):
+                acc = acc_pool.tile([P, 2, D_OUT], F32, tag="acc")
+                for s in range(2):
+                    i = half * 2 + s
+                    for c in range(passes):
+                        nc.tensor.matmul_mx(
+                            out=acc[:, s, :],
+                            lhsT=zn_codes[(j, g, c)][:, i * P : (i + 1) * P].bitcast(FP8X4),
+                            lhsT_scale=zn_scales[(j, g, c)][:, i * P : (i + 1) * P],
+                            rhs=w_codes[:, first_pass + c, :].bitcast(FP8X4),
+                            rhs_scale=w_scales[:, first_pass + c, :],
+                            start=(c == 0),
+                            stop=(c == passes - 1),
+                        )
+                sums[(j, g, half)] = acc
+
+        def gelu_and_store(j, g):
+            result = work.tile([P, GROUP, D_OUT], F32, tag="result")
+            for half in range(GROUP // 2):
+                nc.scalar.activation(out=result[:, half * 2 : half * 2 + 2, :], in_=sums[(j, g, half)][:], func=ACT.Gelu)
+            out_rows = out[j].rearrange("(p i) n -> p i n", i=ROW_TILES)
+            nc.sync.dma_start(out=out_rows[:, g * GROUP : (g + 1) * GROUP, :], in_=result[:])
+
+        n = len(groups)
+        with tc.manual_schedule():
+            statistics(*groups[0])
+            turn_gamma_beta()
+            statistics(*groups[1])
+            quantise_w()
+            for a in range(n + 2):
+                if a < n:
+                    normalise(*groups[a])
+                if a >= 2:
+                    gelu_and_store(*groups[a - 2])
+                if 1 <= a <= n:
+                    quantise(*groups[a - 1])
+                if a < n:
+                    turn(*groups[a])
+                if 1 <= a <= n:
+                    multiply(*groups[a - 1])
+                if a + 2 < n:
+                    statistics(*groups[a + 2])

@@ -32,7 +32,8 @@ TWO_PI_HIGH = 6.28125
 TWO_PI_LOW = 2.0 * math.pi - TWO_PI_HIGH
 SIN_LIMIT = 3.1415925
 
-SCALAR_NORM_TILES = 2
+LOOKAHEAD = 2
+VECTOR_NORM_TILES = 1
 
 FLOPS = 2 * ROWS * D_OUT * (512 + 1024)
 
@@ -194,6 +195,7 @@ def tile_featureprojector_pa_kernel(
         row_shift = {}
         normalised = {}
         planes = {}
+        grouped = {}
         zn_codes = {}
         zn_scales = {}
         sums = {}
@@ -226,7 +228,7 @@ def tile_featureprojector_pa_kernel(
             row_scale[(j, g)] = scale
             row_shift[(j, g)] = shift
 
-        def normalise(j, g):
+        def normalise(j, g, vector_tiles):
             kind = kinds[j]
             d, k = kind["d"], kind["k"]
             scale, shift = row_scale[(j, g)], row_shift[(j, g)]
@@ -237,7 +239,7 @@ def tile_featureprojector_pa_kernel(
                     (xn[:, i, d:k], t2v[:, j * ROW_TILES + g * GROUP + i, :]),
                 ]
                 for dst, src in parts:
-                    if i < SCALAR_NORM_TILES:
+                    if i < GROUP - vector_tiles:
                         nc.scalar.activation(
                             out=dst, in_=src, func=ACT.Identity, scale=scale[:, i : i + 1], bias=shift[:, i : i + 1]
                         )
@@ -276,22 +278,23 @@ def tile_featureprojector_pa_kernel(
                     )
                 planes[(j, g, c)] = zn_planes
 
-        def quantise(j, g):
-            passes = kinds[j]["passes"]
-            grouped = {}
-            for c in range(passes):
-                grouped[c] = work.tile([P, GROUP_COLS, PACK], BF16, tag="grouped", align_bytes=64, name="grouped")
+        def interleave(j, g):
+            for c in range(kinds[j]["passes"]):
+                words_in = work.tile([P, GROUP_COLS, PACK], BF16, tag="grouped", align_bytes=64)
                 nc.vector.tensor_copy(
-                    out=grouped[c][:].rearrange("p (n r) t -> p n t r", r=4),
+                    out=words_in[:].rearrange("p (n r) t -> p n t r", r=4),
                     in_=planes[(j, g, c)][:].rearrange("p t (n r) -> p n t r", r=4),
                 )
-            for c in range(passes):
+                grouped[(j, g, c)] = words_in
+
+        def quantise(j, g):
+            for c in range(kinds[j]["passes"]):
                 zn_codes[(j, g, c)] = work.tile([P, GROUP_COLS], U32, tag="codes", align_bytes=64, name="codes")
                 zn_scales[(j, g, c)] = work.tile([P, GROUP_COLS], U8, tag="scales", align_bytes=64, name="scales")
                 nc.vector.quantize_mx(
                     out=zn_codes[(j, g, c)][:].bitcast(FP8X4),
                     scales=zn_scales[(j, g, c)][:],
-                    in_=grouped[c][:].rearrange("p n t -> p (n t)"),
+                    in_=grouped[(j, g, c)][:].rearrange("p n t -> p (n t)"),
                 )
 
         def multiply(j, g):
@@ -314,11 +317,12 @@ def tile_featureprojector_pa_kernel(
                 sums[(j, g, half)] = acc
 
         def gelu_and_store(j, g):
-            result = work.tile([P, GROUP, D_OUT], F32, tag="result")
-            for half in range(GROUP // 2):
-                nc.scalar.activation(out=result[:, half * 2 : half * 2 + 2, :], in_=sums[(j, g, half)][:], func=ACT.Gelu)
             out_rows = out[j].rearrange("(p i) n -> p i n", i=ROW_TILES)
-            nc.sync.dma_start(out=out_rows[:, g * GROUP : (g + 1) * GROUP, :], in_=result[:])
+            for half in range(GROUP // 2):
+                result = work.tile([P, 2, D_OUT], F32, tag="result")
+                nc.scalar.activation(out=result[:], in_=sums[(j, g, half)][:], func=ACT.Gelu)
+                first_tile = g * GROUP + half * 2
+                nc.sync.dma_start(out=out_rows[:, first_tile : first_tile + 2, :], in_=result[:])
 
         n = len(groups)
         with tc.manual_schedule():
@@ -327,15 +331,17 @@ def tile_featureprojector_pa_kernel(
             statistics(*groups[1])
             quantise_w()
             for a in range(n + 2):
+                if 1 <= a <= n:
+                    interleave(*groups[a - 1])
                 if a < n:
-                    normalise(*groups[a])
-                if a >= 2:
-                    gelu_and_store(*groups[a - 2])
+                    normalise(*groups[a], GROUP if a + LOOKAHEAD >= n else VECTOR_NORM_TILES)
                 if 1 <= a <= n:
                     quantise(*groups[a - 1])
+                if a >= 2:
+                    gelu_and_store(*groups[a - 2])
                 if a < n:
                     turn(*groups[a])
                 if 1 <= a <= n:
                     multiply(*groups[a - 1])
-                if a + 2 < n:
-                    statistics(*groups[a + 2])
+                if a + LOOKAHEAD < n:
+                    statistics(*groups[a + LOOKAHEAD])

@@ -32,8 +32,10 @@ TWO_PI_HIGH = 6.28125
 TWO_PI_LOW = 2.0 * math.pi - TWO_PI_HIGH
 SIN_LIMIT = 3.1415925
 
+GPSIMD_NORM_TILES = 2
 LOOKAHEAD = 2
-VECTOR_NORM_TILES = 1
+LATE_VECTOR_TILES = 2
+LATE_VECTOR_PLANES = 2
 
 FLOPS = 2 * ROWS * D_OUT * (512 + 1024)
 
@@ -79,8 +81,8 @@ def tile_featureprojector_pa_kernel(
     with ExitStack() as stack:
         const = stack.enter_context(tc.tile_pool(name="const", bufs=1))
         x_pool = stack.enter_context(tc.tile_pool(name="x", bufs=1))
-        small = stack.enter_context(tc.tile_pool(name="small", bufs=4))
-        xn_pool = stack.enter_context(tc.tile_pool(name="xn", bufs=2))
+        small = stack.enter_context(tc.tile_pool(name="small", bufs=5))
+        xn_pool = stack.enter_context(tc.tile_pool(name="xn", bufs=3))
         work = stack.enter_context(tc.tile_pool(name="work", bufs=4))
         turned_pool = stack.enter_context(tc.psum_pool(name="turned", bufs=6))
         acc_pool = stack.enter_context(tc.psum_pool(name="acc", bufs=2))
@@ -95,7 +97,7 @@ def tile_featureprojector_pa_kernel(
         b_sb = const.tile([P, T2V], BF16)
         nc.sync.dma_start(out=b_sb[:], in_=b.partition_broadcast(P))
 
-        groups = [(j, g) for j in range(KINDS) for g in range(GROUPS)]
+        groups = [(j, g) for j in (1, 0) for g in range(GROUPS)]
         x_sb = {}
 
         def load_rows(j, g):
@@ -129,40 +131,48 @@ def tile_featureprojector_pa_kernel(
         n_ts = KINDS * ROW_TILES
         n_sin = T2V - 1
         ts_flat = ts_sb[:].rearrange("p j i -> p (j i)")
-        linear = const.tile([P, n_ts], F32)
-        nc.vector.tensor_scalar(
-            out=linear[:], in0=ts_flat, scalar1=w0_sb[:, 0:1], scalar2=b_sb[:, 0:1], op0=ALU.mult, op1=ALU.add
-        )
-        phase = const.tile([P, n_ts, n_sin], F32)
-        nc.vector.tensor_tensor(
-            out=phase[:],
-            in0=ts_flat.unsqueeze(2).to_broadcast([P, n_ts, n_sin]),
-            in1=w_sb[:].unsqueeze(1).to_broadcast([P, n_ts, n_sin]),
-            op=ALU.mult,
-        )
-        nc.vector.tensor_tensor(
-            out=phase[:], in0=phase[:], in1=b_sb[:, 1:T2V].unsqueeze(1).to_broadcast([P, n_ts, n_sin]), op=ALU.add
-        )
-        phase_flat = phase[:].rearrange("p n s -> p (n s)")
-        turns = const.tile([P, n_ts * n_sin], F32)
-        nc.vector.tensor_scalar(
-            out=turns[:], in0=phase_flat, scalar1=1.0 / (2.0 * math.pi), scalar2=ROUND_MAGIC, op0=ALU.mult, op1=ALU.add
-        )
-        nc.vector.tensor_scalar(out=turns[:], in0=turns[:], scalar1=ROUND_MAGIC, scalar2=None, op0=ALU.subtract)
-        reduced = const.tile([P, n_ts, n_sin], F32)
-        reduced_flat = reduced[:].rearrange("p n s -> p (n s)")
-        nc.vector.scalar_tensor_tensor(
-            out=reduced_flat, in0=turns[:], scalar=-TWO_PI_HIGH, in1=phase_flat, op0=ALU.mult, op1=ALU.add
-        )
-        nc.vector.scalar_tensor_tensor(
-            out=reduced_flat, in0=turns[:], scalar=-TWO_PI_LOW, in1=reduced_flat, op0=ALU.mult, op1=ALU.add
-        )
-        nc.vector.tensor_scalar(
-            out=reduced_flat, in0=reduced_flat, scalar1=-SIN_LIMIT, scalar2=SIN_LIMIT, op0=ALU.max, op1=ALU.min
-        )
         t2v = const.tile([P, n_ts, T2V], F32)
-        nc.scalar.activation(out=t2v[:, :, 1:T2V], in_=reduced[:], func=ACT.Sin)
-        nc.scalar.copy(out=t2v[:, :, 0:1], in_=linear[:].unsqueeze(2))
+
+        def time2vec(first, count):
+            ts_part = ts_flat[:, first : first + count]
+            linear = small.tile([P, count], F32, tag="linear")
+            nc.vector.tensor_scalar(
+                out=linear[:], in0=ts_part, scalar1=w0_sb[:, 0:1], scalar2=b_sb[:, 0:1], op0=ALU.mult, op1=ALU.add
+            )
+            phase = small.tile([P, count, n_sin], F32, tag="phase")
+            nc.vector.tensor_tensor(
+                out=phase[:],
+                in0=ts_part.unsqueeze(2).to_broadcast([P, count, n_sin]),
+                in1=w_sb[:].unsqueeze(1).to_broadcast([P, count, n_sin]),
+                op=ALU.mult,
+            )
+            nc.vector.tensor_tensor(
+                out=phase[:], in0=phase[:], in1=b_sb[:, 1:T2V].unsqueeze(1).to_broadcast([P, count, n_sin]), op=ALU.add
+            )
+            phase_flat = phase[:].rearrange("p n s -> p (n s)")
+            turns = small.tile([P, count * n_sin], F32, tag="turns")
+            nc.vector.tensor_scalar(
+                out=turns[:],
+                in0=phase_flat,
+                scalar1=1.0 / (2.0 * math.pi),
+                scalar2=ROUND_MAGIC,
+                op0=ALU.mult,
+                op1=ALU.add,
+            )
+            nc.vector.tensor_scalar(out=turns[:], in0=turns[:], scalar1=ROUND_MAGIC, scalar2=None, op0=ALU.subtract)
+            reduced = small.tile([P, count, n_sin], F32, tag="reduced")
+            reduced_flat = reduced[:].rearrange("p n s -> p (n s)")
+            nc.vector.scalar_tensor_tensor(
+                out=reduced_flat, in0=turns[:], scalar=-TWO_PI_HIGH, in1=phase_flat, op0=ALU.mult, op1=ALU.add
+            )
+            nc.vector.scalar_tensor_tensor(
+                out=reduced_flat, in0=turns[:], scalar=-TWO_PI_LOW, in1=reduced_flat, op0=ALU.mult, op1=ALU.add
+            )
+            nc.vector.tensor_scalar(
+                out=reduced_flat, in0=reduced_flat, scalar1=-SIN_LIMIT, scalar2=SIN_LIMIT, op0=ALU.max, op1=ALU.min
+            )
+            nc.scalar.activation(out=t2v[:, first : first + count, 1:T2V], in_=reduced[:], func=ACT.Sin)
+            nc.scalar.copy(out=t2v[:, first : first + count, 0:1], in_=linear[:].unsqueeze(2))
 
         neg_half = const.tile([P, GROUP], F32)
         nc.vector.memset(neg_half[:], -0.5)
@@ -192,10 +202,10 @@ def tile_featureprojector_pa_kernel(
                 )
 
         row_scale = {}
+        row_neg_mean = {}
         row_shift = {}
         normalised = {}
         planes = {}
-        grouped = {}
         zn_codes = {}
         zn_scales = {}
         sums = {}
@@ -219,19 +229,20 @@ def tile_featureprojector_pa_kernel(
             )
             scale = small.tile([P, GROUP], F32, tag="scale")
             nc.gpsimd.tensor_tensor(out=scale[:], in0=var_eps[:], in1=neg_half[:], op=ALU.pow)
-            mean_scaled = small.tile([P, GROUP], F32, tag="mean_scaled")
-            nc.gpsimd.tensor_tensor(out=mean_scaled[:], in0=mean_var[:, :, 0], in1=scale[:], op=ALU.mult)
-            shift = small.tile([P, GROUP], F32, tag="shift")
+            neg_mean = small.tile([P, GROUP], F32, tag="neg_mean")
             nc.gpsimd.tensor_scalar(
-                out=shift[:], in0=mean_scaled[:], scalar1=-1.0, scalar2=0.0, op0=ALU.mult, op1=ALU.add
+                out=neg_mean[:], in0=mean_var[:, :, 0], scalar1=-1.0, scalar2=0.0, op0=ALU.mult, op1=ALU.add
             )
+            shift = small.tile([P, GROUP], F32, tag="shift")
+            nc.gpsimd.tensor_tensor(out=shift[:], in0=neg_mean[:], in1=scale[:], op=ALU.mult)
             row_scale[(j, g)] = scale
+            row_neg_mean[(j, g)] = neg_mean
             row_shift[(j, g)] = shift
 
         def normalise(j, g, vector_tiles):
             kind = kinds[j]
             d, k = kind["d"], kind["k"]
-            scale, shift = row_scale[(j, g)], row_shift[(j, g)]
+            scale, neg_mean, shift = row_scale[(j, g)], row_neg_mean[(j, g)], row_shift[(j, g)]
             xn = xn_pool.tile([P, GROUP, k], F32, tag="xn")
             for i in range(GROUP):
                 parts = [
@@ -239,7 +250,16 @@ def tile_featureprojector_pa_kernel(
                     (xn[:, i, d:k], t2v[:, j * ROW_TILES + g * GROUP + i, :]),
                 ]
                 for dst, src in parts:
-                    if i < GROUP - vector_tiles:
+                    if i < GPSIMD_NORM_TILES:
+                        nc.gpsimd.tensor_scalar(
+                            out=dst,
+                            in0=src,
+                            scalar1=neg_mean[:, i : i + 1],
+                            scalar2=scale[:, i : i + 1],
+                            op0=ALU.add,
+                            op1=ALU.mult,
+                        )
+                    elif i < GROUP - vector_tiles:
                         nc.scalar.activation(
                             out=dst, in_=src, func=ACT.Identity, scale=scale[:, i : i + 1], bias=shift[:, i : i + 1]
                         )
@@ -247,14 +267,14 @@ def tile_featureprojector_pa_kernel(
                         nc.vector.tensor_scalar(
                             out=dst,
                             in0=src,
-                            scalar1=scale[:, i : i + 1],
-                            scalar2=shift[:, i : i + 1],
-                            op0=ALU.mult,
-                            op1=ALU.add,
+                            scalar1=neg_mean[:, i : i + 1],
+                            scalar2=scale[:, i : i + 1],
+                            op0=ALU.add,
+                            op1=ALU.mult,
                         )
             normalised[(j, g)] = xn
 
-        def turn(j, g):
+        def turn(j, g, vector_planes):
             kind = kinds[j]
             xn = normalised[(j, g)]
             for c in range(kind["passes"]):
@@ -269,32 +289,32 @@ def tile_featureprojector_pa_kernel(
                             identity[:],
                         )
                     col = kind["first"] + tile_in_kind
-                    nc.scalar.activation(
-                        out=zn_planes[:, t, :],
-                        in_=turned[:],
-                        func=ACT.Identity,
-                        scale=gamma_beta[:, col : col + 1],
-                        bias=gamma_beta[:, all_tiles + col : all_tiles + col + 1],
-                    )
+                    gamma = gamma_beta[:, col : col + 1]
+                    beta = gamma_beta[:, all_tiles + col : all_tiles + col + 1]
+                    if t < PACK - vector_planes:
+                        nc.scalar.activation(out=zn_planes[:, t, :], in_=turned[:], func=ACT.Identity, scale=gamma, bias=beta)
+                    else:
+                        nc.vector.tensor_scalar(
+                            out=zn_planes[:, t, :], in0=turned[:], scalar1=gamma, scalar2=beta, op0=ALU.mult, op1=ALU.add
+                        )
                 planes[(j, g, c)] = zn_planes
 
-        def interleave(j, g):
-            for c in range(kinds[j]["passes"]):
-                words_in = work.tile([P, GROUP_COLS, PACK], BF16, tag="grouped", align_bytes=64)
+        def quantise(j, g):
+            passes = kinds[j]["passes"]
+            grouped = {}
+            for c in range(passes):
+                grouped[c] = work.tile([P, GROUP_COLS, PACK], BF16, tag="grouped", align_bytes=64, name="grouped")
                 nc.vector.tensor_copy(
-                    out=words_in[:].rearrange("p (n r) t -> p n t r", r=4),
+                    out=grouped[c][:].rearrange("p (n r) t -> p n t r", r=4),
                     in_=planes[(j, g, c)][:].rearrange("p t (n r) -> p n t r", r=4),
                 )
-                grouped[(j, g, c)] = words_in
-
-        def quantise(j, g):
-            for c in range(kinds[j]["passes"]):
+            for c in range(passes):
                 zn_codes[(j, g, c)] = work.tile([P, GROUP_COLS], U32, tag="codes", align_bytes=64, name="codes")
                 zn_scales[(j, g, c)] = work.tile([P, GROUP_COLS], U8, tag="scales", align_bytes=64, name="scales")
                 nc.vector.quantize_mx(
                     out=zn_codes[(j, g, c)][:].bitcast(FP8X4),
                     scales=zn_scales[(j, g, c)][:],
-                    in_=grouped[(j, g, c)][:].rearrange("p n t -> p (n t)"),
+                    in_=grouped[c][:].rearrange("p n t -> p (n t)"),
                 )
 
         def multiply(j, g):
@@ -325,23 +345,22 @@ def tile_featureprojector_pa_kernel(
                 nc.sync.dma_start(out=out_rows[:, first_tile : first_tile + 2, :], in_=result[:])
 
         n = len(groups)
-        with tc.manual_schedule():
-            statistics(*groups[0])
-            turn_gamma_beta()
-            statistics(*groups[1])
-            quantise_w()
-            for a in range(n + 2):
-                if 1 <= a <= n:
-                    interleave(*groups[a - 1])
-                if a < n:
-                    normalise(*groups[a], GROUP if a + LOOKAHEAD >= n else VECTOR_NORM_TILES)
-                if 1 <= a <= n:
-                    quantise(*groups[a - 1])
-                if a >= 2:
-                    gelu_and_store(*groups[a - 2])
-                if a < n:
-                    turn(*groups[a])
-                if 1 <= a <= n:
-                    multiply(*groups[a - 1])
-                if a + LOOKAHEAD < n:
-                    statistics(*groups[a + LOOKAHEAD])
+        time2vec(0, n_ts)
+        for a in range(-1 - LOOKAHEAD, n + 2):
+            ahead = a + 1
+            if 0 <= ahead < n:
+                normalise(*groups[ahead], LATE_VECTOR_TILES if ahead + LOOKAHEAD >= n else 0)
+            if 0 <= a - 2:
+                gelu_and_store(*groups[a - 2])
+            if 0 <= a - 1 < n:
+                quantise(*groups[a - 1])
+            if 0 <= a < n:
+                turn(*groups[a], LATE_VECTOR_PLANES if a + LOOKAHEAD >= n else 0)
+            if 0 <= a - 1 < n:
+                multiply(*groups[a - 1])
+            if ahead + LOOKAHEAD < n:
+                statistics(*groups[ahead + LOOKAHEAD])
+            if ahead + LOOKAHEAD == 0:
+                turn_gamma_beta()
+            if ahead + LOOKAHEAD == 1:
+                quantise_w()

@@ -32,9 +32,9 @@ TWO_PI_HIGH = 6.28125
 TWO_PI_LOW = 2.0 * math.pi - TWO_PI_HIGH
 SIN_LIMIT = 3.1415925
 
-GPSIMD_NORM_TILES = 2
+VECTOR_NORM_TILES = 2
 LOOKAHEAD = 2
-LATE_VECTOR_TILES = 2
+LATE_VECTOR_TILES = 4
 LATE_VECTOR_PLANES = 2
 
 FLOPS = 2 * ROWS * D_OUT * (512 + 1024)
@@ -250,16 +250,7 @@ def tile_featureprojector_pa_kernel(
                     (xn[:, i, d:k], t2v[:, j * ROW_TILES + g * GROUP + i, :]),
                 ]
                 for dst, src in parts:
-                    if i < GPSIMD_NORM_TILES:
-                        nc.gpsimd.tensor_scalar(
-                            out=dst,
-                            in0=src,
-                            scalar1=neg_mean[:, i : i + 1],
-                            scalar2=scale[:, i : i + 1],
-                            op0=ALU.add,
-                            op1=ALU.mult,
-                        )
-                    elif i < GROUP - vector_tiles:
+                    if i < GROUP - vector_tiles:
                         nc.scalar.activation(
                             out=dst, in_=src, func=ACT.Identity, scale=scale[:, i : i + 1], bias=shift[:, i : i + 1]
                         )
@@ -349,7 +340,7 @@ def tile_featureprojector_pa_kernel(
         for a in range(-1 - LOOKAHEAD, n + 2):
             ahead = a + 1
             if 0 <= ahead < n:
-                normalise(*groups[ahead], LATE_VECTOR_TILES if ahead + LOOKAHEAD >= n else 0)
+                normalise(*groups[ahead], LATE_VECTOR_TILES if ahead + LOOKAHEAD >= n else VECTOR_NORM_TILES)
             if 0 <= a - 2:
                 gelu_and_store(*groups[a - 2])
             if 0 <= a - 1 < n:

@@ -336,22 +336,23 @@ def tile_featureprojector_pa_kernel(
                 nc.sync.dma_start(out=out_rows[:, first_tile : first_tile + 2, :], in_=result[:])
 
         n = len(groups)
-        time2vec(0, n_ts)
-        for a in range(-1 - LOOKAHEAD, n + 2):
-            ahead = a + 1
-            if 0 <= ahead < n:
-                normalise(*groups[ahead], LATE_VECTOR_TILES if ahead + LOOKAHEAD >= n else VECTOR_NORM_TILES)
-            if 0 <= a - 2:
-                gelu_and_store(*groups[a - 2])
-            if 0 <= a - 1 < n:
-                quantise(*groups[a - 1])
-            if 0 <= a < n:
-                turn(*groups[a], LATE_VECTOR_PLANES if a + LOOKAHEAD >= n else 0)
-            if 0 <= a - 1 < n:
-                multiply(*groups[a - 1])
-            if ahead + LOOKAHEAD < n:
-                statistics(*groups[ahead + LOOKAHEAD])
-            if ahead + LOOKAHEAD == 0:
-                turn_gamma_beta()
-            if ahead + LOOKAHEAD == 1:
-                quantise_w()
+        with tc.manual_schedule():
+            time2vec(0, n_ts)
+            for a in range(-1 - LOOKAHEAD, n + 2):
+                ahead = a + 1
+                if 0 <= ahead < n:
+                    normalise(*groups[ahead], LATE_VECTOR_TILES if ahead + LOOKAHEAD >= n else VECTOR_NORM_TILES)
+                if 0 <= a - 2:
+                    gelu_and_store(*groups[a - 2])
+                if 0 <= a - 1 < n:
+                    quantise(*groups[a - 1])
+                if 0 <= a < n:
+                    turn(*groups[a], LATE_VECTOR_PLANES if a + LOOKAHEAD >= n else 0)
+                if 0 <= a - 1 < n:
+                    multiply(*groups[a - 1])
+                if ahead + LOOKAHEAD < n:
+                    statistics(*groups[ahead + LOOKAHEAD])
+                if ahead + LOOKAHEAD == 0:
+                    turn_gamma_beta()
+                if ahead + LOOKAHEAD == 1:
+                    quantise_w()

from contextlib import ExitStack
import math

import concourse.mybir as mybir
from concourse.masks import make_identity

F32 = mybir.dt.float32
BF16 = mybir.dt.bfloat16
U32 = mybir.dt.uint32
U8 = mybir.dt.uint8
FP8X4 = mybir.dt.float8_e4m3fn_x4
ACT = mybir.ActivationFunctionType
ALU = mybir.AluOpType

P = 128
PACK = 4
K_PASS = P * PACK
ROWS = 2048
ROW_TILES = ROWS // P
GROUP = 4
GROUPS = ROW_TILES // GROUP
GROUP_COLS = GROUP * P
T2V = 12
D_OUT = 256
LN_EPS = 1e-5
BN_MAX = 512
BN_DIM = 6
KINDS = 2

ROUND_MAGIC = 12582912.0
TWO_PI_HIGH = 6.28125
TWO_PI_LOW = 2.0 * math.pi - TWO_PI_HIGH
SIN_LIMIT = 3.1415925

VECTOR_NORM_TILES = 2
LOOKAHEAD = 2
LATE_VECTOR_TILES = 4
LATE_VECTOR_PLANES = 2

FLOPS = 2 * ROWS * D_OUT * (512 + 1024)


def tile_featureprojector_pa_kernel(
    tc,
    x_bill,
    ts_bill,
    x_bill_version,
    ts_bill_version,
    w0,
    w,
    b,
    gamma_bill,
    beta_bill,
    W_bill,
    gamma_bill_version,
    beta_bill_version,
    W_bill_version,
    out,
):
    nc = tc.nc
    kinds = [
        {"x": x_bill, "ts": ts_bill, "gamma": gamma_bill, "beta": beta_bill, "W": W_bill, "first": 0},
        {
            "x": x_bill_version,
            "ts": ts_bill_version,
            "gamma": gamma_bill_version,
            "beta": beta_bill_version,
            "W": W_bill_version,
            "first": 4,
        },
    ]
    for kind in kinds:
        kind["d"] = kind["x"].shape[1]
        kind["k"] = kind["d"] + T2V
        kind["tiles"] = kind["k"] // P
        kind["passes"] = kind["k"] // K_PASS
        kind["chunks"] = (kind["d"] + BN_MAX - 1) // BN_MAX
    all_tiles = sum(kind["tiles"] for kind in kinds)
    all_passes = sum(kind["passes"] for kind in kinds)

    with ExitStack() as stack:
        const = stack.enter_context(tc.tile_pool(name="const", bufs=1))
        x_pool = stack.enter_context(tc.tile_pool(name="x", bufs=1))
        small = stack.enter_context(tc.tile_pool(name="small", bufs=5))
        xn_pool = stack.enter_context(tc.tile_pool(name="xn", bufs=3))
        work = stack.enter_context(tc.tile_pool(name="work", bufs=4))
        turned_pool = stack.enter_context(tc.psum_pool(name="turned", bufs=6))
        acc_pool = stack.enter_context(tc.psum_pool(name="acc", bufs=2))

        ts_sb = const.tile([P, KINDS, ROW_TILES], BF16)
        for j, kind in enumerate(kinds):
            nc.sync.dma_start(out=ts_sb[:, j, :], in_=kind["ts"].rearrange("(p i) -> p i", i=ROW_TILES))
        w0_sb = const.tile([P, 1], BF16)
        nc.sync.dma_start(out=w0_sb[:], in_=w0.partition_broadcast(P))
        w_sb = const.tile([P, T2V - 1], BF16)
        nc.sync.dma_start(out=w_sb[:], in_=w.partition_broadcast(P))
        b_sb = const.tile([P, T2V], BF16)
        nc.sync.dma_start(out=b_sb[:], in_=b.partition_broadcast(P))

        groups = [(j, g) for j in (1, 0) for g in range(GROUPS)]
        x_sb = {}

        def load_rows(j, g):
            x_tile = x_pool.tile([P, GROUP, kinds[j]["d"]], BF16, name="x_%d_%d" % (j, g))
            rows = kinds[j]["x"].rearrange("(p i) d -> p i d", i=ROW_TILES)
            nc.sync.dma_start(out=x_tile[:], in_=rows[:, g * GROUP : (g + 1) * GROUP, :])
            x_sb[(j, g)] = x_tile

        load_rows(*groups[0])

        gb_rows = const.tile([P, P], BF16)
        nc.vector.memset(gb_rows[:], 0.0)
        w_raw = const.tile([P, all_tiles, D_OUT], BF16)
        for kind in kinds:
            first, tiles = kind["first"], kind["tiles"]
            nc.sync.dma_start(out=gb_rows[first : first + tiles, :], in_=kind["gamma"].rearrange("(t p) -> t p", p=P))
            nc.sync.dma_start(
                out=gb_rows[all_tiles + first : all_tiles + first + tiles, :],
                in_=kind["beta"].rearrange("(t p) -> t p", p=P),
            )
        for kind in kinds:
            first, tiles = kind["first"], kind["tiles"]
            nc.sync.dma_start(out=w_raw[:, first : first + tiles, :], in_=kind["W"].rearrange("(t p) n -> p t n", p=P))

        for j, g in groups[1:]:
            load_rows(j, g)

        identity = const.tile([P, P], F32)
        make_identity(nc, identity[:])

        n_ts = KINDS * ROW_TILES
        n_sin = T2V - 1
        ts_flat = ts_sb[:].rearrange("p j i -> p (j i)")
        t2v = const.tile([P, n_ts, T2V], F32)

        def time2vec(first, count):
            ts_part = ts_flat[:, first : first + count]
            linear = small.tile([P, count], F32, tag="linear")
            nc.vector.tensor_scalar(
                out=linear[:], in0=ts_part, scalar1=w0_sb[:, 0:1], scalar2=b_sb[:, 0:1], op0=ALU.mult, op1=ALU.add
            )
            phase = small.tile([P, count, n_sin], F32, tag="phase")
            nc.vector.tensor_tensor(
                out=phase[:],
                in0=ts_part.unsqueeze(2).to_broadcast([P, count, n_sin]),
                in1=w_sb[:].unsqueeze(1).to_broadcast([P, count, n_sin]),
                op=ALU.mult,
            )
            nc.vector.tensor_tensor(
                out=phase[:], in0=phase[:], in1=b_sb[:, 1:T2V].unsqueeze(1).to_broadcast([P, count, n_sin]), op=ALU.add
            )
            phase_flat = phase[:].rearrange("p n s -> p (n s)")
            turns = small.tile([P, count * n_sin], F32, tag="turns")
            nc.vector.tensor_scalar(
                out=turns[:],
                in0=phase_flat,
                scalar1=1.0 / (2.0 * math.pi),
                scalar2=ROUND_MAGIC,
                op0=ALU.mult,
                op1=ALU.add,
            )
            nc.vector.tensor_scalar(out=turns[:], in0=turns[:], scalar1=ROUND_MAGIC, scalar2=None, op0=ALU.subtract)
            reduced = small.tile([P, count, n_sin], F32, tag="reduced")
            reduced_flat = reduced[:].rearrange("p n s -> p (n s)")
            nc.vector.scalar_tensor_tensor(
                out=reduced_flat, in0=turns[:], scalar=-TWO_PI_HIGH, in1=phase_flat, op0=ALU.mult, op1=ALU.add
            )
            nc.vector.scalar_tensor_tensor(
                out=reduced_flat, in0=turns[:], scalar=-TWO_PI_LOW, in1=reduced_flat, op0=ALU.mult, op1=ALU.add
            )
            nc.vector.tensor_scalar(
                out=reduced_flat, in0=reduced_flat, scalar1=-SIN_LIMIT, scalar2=SIN_LIMIT, op0=ALU.max, op1=ALU.min
            )
            nc.scalar.activation(out=t2v[:, first : first + count, 1:T2V], in_=reduced[:], func=ACT.Sin)
            nc.scalar.copy(out=t2v[:, first : first + count, 0:1], in_=linear[:].unsqueeze(2))

        neg_half = const.tile([P, GROUP], F32)
        nc.vector.memset(neg_half[:], -0.5)

        gamma_beta = const.tile([P, 2 * all_tiles], F32)
        w_codes = const.tile([P, all_passes, D_OUT], U32, align_bytes=64)
        w_scales = const.tile([P, all_passes, D_OUT], U8, align_bytes=64)

        def turn_gamma_beta():
            gb_rows_f32 = const.tile([P, P], F32)
            nc.vector.tensor_copy(out=gb_rows_f32[:], in_=gb_rows[:])
            gb_turned = turned_pool.tile([P, GROUP_COLS], F32, tag="turned")
            nc.tensor.transpose(gb_turned[:, 0:P], gb_rows_f32[:], identity[:])
            nc.vector.tensor_copy(out=gamma_beta[:], in_=gb_turned[:, 0 : 2 * all_tiles])

        def quantise_w():
            w_grouped = const.tile([P, all_passes, D_OUT, PACK], BF16, align_bytes=64)
            for c in range(all_passes):
                nc.scalar.copy(
                    out=w_grouped[:, c, :, :], in_=w_raw[:, c * PACK : (c + 1) * PACK, :].rearrange("p t n -> p n t")
                )
            for c in range(all_passes):
                nc.vector.quantize_mx(
                    out=w_codes[:, c, :].bitcast(FP8X4),
                    scales=w_scales[:, c, :],
                    in_=w_grouped[:, c, :, :].rearrange("p n t -> p (n t)"),
                )

        row_scale = {}
        row_neg_mean = {}
        row_shift = {}
        normalised = {}
        planes = {}
        zn_codes = {}
        zn_scales = {}
        sums = {}

        def statistics(j, g):
            kind = kinds[j]
            chunks = kind["chunks"]
            width = kind["d"] // chunks
            stats = small.tile([P, GROUP, chunks + 1, BN_DIM], F32, tag="stats")
            mean_var = small.tile([P, GROUP, 2], F32, tag="mean_var")
            for i in range(GROUP):
                for h in range(chunks):
                    nc.vector.bn_stats(out=stats[:, i, h, :], in_=x_sb[(j, g)][:, i, h * width : (h + 1) * width])
            for i in range(GROUP):
                nc.vector.bn_stats(out=stats[:, i, chunks, :], in_=t2v[:, j * ROW_TILES + g * GROUP + i, :])
            for i in range(GROUP):
                nc.vector.bn_aggr(out=mean_var[:, i, :], in_=stats[:, i, :, :].rearrange("p h s -> p (h s)"))
            var_eps = small.tile([P, GROUP], F32, tag="var_eps")
            nc.gpsimd.tensor_scalar(
                out=var_eps[:], in0=mean_var[:, :, 1], scalar1=LN_EPS, scalar2=1.0, op0=ALU.add, op1=ALU.mult
            )
            scale = small.tile([P, GROUP], F32, tag="scale")
            nc.gpsimd.tensor_tensor(out=scale[:], in0=var_eps[:], in1=neg_half[:], op=ALU.pow)
            neg_mean = small.tile([P, GROUP], F32, tag="neg_mean")
            nc.gpsimd.tensor_scalar(
                out=neg_mean[:], in0=mean_var[:, :, 0], scalar1=-1.0, scalar2=0.0, op0=ALU.mult, op1=ALU.add
            )
            shift = small.tile([P, GROUP], F32, tag="shift")
            nc.gpsimd.tensor_tensor(out=shift[:], in0=neg_mean[:], in1=scale[:], op=ALU.mult)
            row_scale[(j, g)] = scale
            row_neg_mean[(j, g)] = neg_mean
            row_shift[(j, g)] = shift

        def normalise(j, g, vector_tiles):
            kind = kinds[j]
            d, k = kind["d"], kind["k"]
            scale, neg_mean, shift = row_scale[(j, g)], row_neg_mean[(j, g)], row_shift[(j, g)]
            xn = xn_pool.tile([P, GROUP, k], F32, tag="xn")
            for i in range(GROUP):
                parts = [
                    (xn[:, i, 0:d], x_sb[(j, g)][:, i, :]),
                    (xn[:, i, d:k], t2v[:, j * ROW_TILES + g * GROUP + i, :]),
                ]
                for dst, src in parts:
                    if i < GROUP - vector_tiles:
                        nc.scalar.activation(
                            out=dst, in_=src, func=ACT.Identity, scale=scale[:, i : i + 1], bias=shift[:, i : i + 1]
                        )
                    else:
                        nc.vector.tensor_scalar(
                            out=dst,
                            in0=src,
                            scalar1=neg_mean[:, i : i + 1],
                            scalar2=scale[:, i : i + 1],
                            op0=ALU.add,
                            op1=ALU.mult,
                        )
            normalised[(j, g)] = xn

        def turn(j, g, vector_planes):
            kind = kinds[j]
            xn = normalised[(j, g)]
            for c in range(kind["passes"]):
                zn_planes = work.tile([P, PACK, GROUP_COLS], BF16, tag="zn_planes")
                for t in range(PACK):
                    tile_in_kind = c * PACK + t
                    turned = turned_pool.tile([P, GROUP_COLS], F32, tag="turned")
                    for i in range(GROUP):
                        nc.tensor.transpose(
                            turned[:, i * P : (i + 1) * P],
                            xn[:, i, tile_in_kind * P : (tile_in_kind + 1) * P],
                            identity[:],
                        )
                    col = kind["first"] + tile_in_kind
                    gamma = gamma_beta[:, col : col + 1]
                    beta = gamma_beta[:, all_tiles + col : all_tiles + col + 1]
                    if t < PACK - vector_planes:
                        nc.scalar.activation(out=zn_planes[:, t, :], in_=turned[:], func=ACT.Identity, scale=gamma, bias=beta)
                    else:
                        nc.vector.tensor_scalar(
                            out=zn_planes[:, t, :], in0=turned[:], scalar1=gamma, scalar2=beta, op0=ALU.mult, op1=ALU.add
                        )
                planes[(j, g, c)] = zn_planes

        def quantise(j, g):
            passes = kinds[j]["passes"]
            grouped = {}
            for c in range(passes):
                grouped[c] = work.tile([P, GROUP_COLS, PACK], BF16, tag="grouped", align_bytes=64, name="grouped")
                nc.vector.tensor_copy(
                    out=grouped[c][:].rearrange("p (n r) t -> p n t r", r=4),
                    in_=planes[(j, g, c)][:].rearrange("p t (n r) -> p n t r", r=4),
                )
            for c in range(passes):
                zn_codes[(j, g, c)] = work.tile([P, GROUP_COLS], U32, tag="codes", align_bytes=64, name="codes")
                zn_scales[(j, g, c)] = work.tile([P, GROUP_COLS], U8, tag="scales", align_bytes=64, name="scales")
                nc.vector.quantize_mx(
                    out=zn_codes[(j, g, c)][:].bitcast(FP8X4),
                    scales=zn_scales[(j, g, c)][:],
                    in_=grouped[c][:].rearrange("p n t -> p (n t)"),
                )

        def multiply(j, g):
            passes = kinds[j]["passes"]
            first_pass = kinds[j]["first"] // PACK
            for half in range(GROUP // 2):
                acc = acc_pool.tile([P, 2, D_OUT], F32, tag="acc")
                for s in range(2):
                    i = half * 2 + s
                    for c in range(passes):
                        nc.tensor.matmul_mx(
                            out=acc[:, s, :],
                            lhsT=zn_codes[(j, g, c)][:, i * P : (i + 1) * P].bitcast(FP8X4),
                            lhsT_scale=zn_scales[(j, g, c)][:, i * P : (i + 1) * P],
                            rhs=w_codes[:, first_pass + c, :].bitcast(FP8X4),
                            rhs_scale=w_scales[:, first_pass + c, :],
                            start=(c == 0),
                            stop=(c == passes - 1),
                        )
                sums[(j, g, half)] = acc

        def gelu_and_store(j, g):
            out_rows = out[j].rearrange("(p i) n -> p i n", i=ROW_TILES)
            for half in range(GROUP // 2):
                result = work.tile([P, 2, D_OUT], F32, tag="result")
                nc.scalar.activation(out=result[:], in_=sums[(j, g, half)][:], func=ACT.Gelu)
                first_tile = g * GROUP + half * 2
                nc.sync.dma_start(out=out_rows[:, first_tile : first_tile + 2, :], in_=result[:])

        n = len(groups)
        with tc.manual_schedule():
            time2vec(0, n_ts)
            for a in range(-1 - LOOKAHEAD, n + 2):
                ahead = a + 1
                if 0 <= ahead < n:
                    normalise(*groups[ahead], LATE_VECTOR_TILES if ahead + LOOKAHEAD >= n else VECTOR_NORM_TILES)
                if 0 <= a - 2:
                    gelu_and_store(*groups[a - 2])
                if 0 <= a - 1 < n:
                    quantise(*groups[a - 1])
                if 0 <= a < n:
                    turn(*groups[a], LATE_VECTOR_PLANES if a + LOOKAHEAD >= n else 0)
                if 0 <= a - 1 < n:
                    multiply(*groups[a - 1])
                if ahead + LOOKAHEAD < n:
                    statistics(*groups[ahead + LOOKAHEAD])
                if ahead + LOOKAHEAD == 0:
                    turn_gamma_beta()
                if ahead + LOOKAHEAD == 1:
                    quantise_w()
